import numpy as np
import ml_dtypes


def mxq(x, axis, fmt="e4m3"):
    dtype, down = {"e4m3": (ml_dtypes.float8_e4m3fn, 7), "e5m2": (ml_dtypes.float8_e5m2, 14)}[fmt]
    v = np.moveaxis(np.asarray(x, np.float32).astype(ml_dtypes.bfloat16).astype(np.float64), axis, -1)
    blocks = v.reshape(v.shape[:-1] + (-1, 32))
    amax = np.abs(blocks).max(-1, keepdims=True)
    byte = np.maximum(np.where(amax > 0, np.frexp(amax)[1] - 1 + 127, 0) - down, 1)
    scale = np.exp2(byte - 127.0)
    codes = (blocks / scale).astype(np.float32).astype(dtype).astype(np.float64)
    return np.moveaxis((codes * scale).reshape(v.shape), -1, axis)


WIDE = False


def mx_kscale(k):
    if not WIDE:
        return np.ones(k)
    levels = np.array([20, -20, 10, -10, 0])
    a = np.random.permutation(np.resize(levels, k // 512 * 4)).reshape(k // 512, 4)
    idx = np.arange(k)
    return np.exp2(a[idx // 512, idx % 128 // 32])


BF16 = ml_dtypes.bfloat16


def bf(x):
    return np.asarray(x, np.float32).astype(BF16)


def f64(x):
    return np.asarray(x).astype(np.float64)


B, N, I, O = 512, 12, 512, 512
WS = 0.7 / np.sqrt(I)
GS = 16.0


def setup_inputs():
    u = mx_kscale(O)
    x = np.random.standard_normal((B, N, I)).reshape(B, N * I)
    w_self = np.random.standard_normal((N, O, I)) * WS / u[:, None]
    w_parent = np.random.standard_normal((N - 1, O, I)) * WS / u[:, None]
    bias = np.random.standard_normal(N * O) * 0.5
    g = np.random.standard_normal((B, N, O)) * np.exp2(np.random.randint(-12, 1, (B, 1, 1))) * GS * u
    return {"x": bf(x), "w_self": bf(w_self), "w_parent": bf(w_parent), "bias": bf(bias),
            "grad_out": bf(g.reshape(B, N * O))}


def reference(x, w_self, w_parent, bias, grad_out):
    gq = mxq(f64(grad_out).reshape(B, N, O).transpose(1, 0, 2), 2, "e5m2")
    d_self = gq @ mxq(f64(w_self), 1, "e4m3")
    d_par = gq[1:] @ mxq(f64(w_parent), 1, "e4m3")
    d = np.concatenate([d_self[:-1] + d_par, d_self[-1:]], 0)
    return d.transpose(1, 0, 2).reshape(B, N * I)

@@ -1,0 +1,171 @@
+import concourse.mybir as mybir
+from concourse.masks import make_identity
+
+BF16 = mybir.dt.bfloat16
+F32 = mybir.dt.float32
+U32 = mybir.dt.uint32
+U8 = mybir.dt.uint8
+E5M2_X4 = mybir.dt.float8_e5m2_x4
+E4M3_X4 = mybir.dt.float8_e4m3fn_x4
+
+P = 128
+PACK = 4
+BATCH = 512
+JOINTS = 12
+CH = 512
+ROW_TILES = BATCH // P
+LAST = JOINTS - 1
+
+WORDS = PACK // 2
+JOINTS_PER_BANK = 2
+JOINTS_PER_QUANTISE = 4
+JOINTS_PER_STORE = 2
+WEIGHT_BUFS = 8
+
+FLOPS = 2 * BATCH * CH * CH * (2 * JOINTS - 1)
+BYTES = 2 * BATCH * JOINTS * CH + 2 * (2 * JOINTS - 1) * CH * CH + 4 * BATCH * JOINTS * CH
+
+
+def tile_skeletonlinear_pa_kernel(tc, x, w_self, w_parent, bias, grad_out, out):
+    nc = tc.nc
+
+    with tc.tile_pool(name="keep", bufs=1) as keep, tc.tile_pool(
+        name="weights", bufs=WEIGHT_BUFS
+    ) as weights, tc.tile_pool(name="packed", bufs=3) as packed, tc.psum_pool(
+        name="psum", bufs=8
+    ) as psum:
+        identity = keep.tile([P, P], F32)
+        make_identity(nc, identity[:])
+
+        g_codes = keep.tile([P, ROW_TILES, JOINTS, P], U32, align_bytes=64)
+        g_scales = keep.tile([P, ROW_TILES, JOINTS, P], U8, align_bytes=64)
+
+        def load_weights(n):
+            w_rows = weights.tile([P, 2, PACK, CH], BF16, name="w_rows")
+            nc.sync.dma_start(
+                out=w_rows[:, 0], in_=w_self[n].rearrange("(p j) i -> p j i", j=PACK)
+            )
+            if n < LAST:
+                nc.sync.dma_start(
+                    out=w_rows[:, 1], in_=w_parent[n].rearrange("(p j) i -> p j i", j=PACK)
+                )
+            return w_rows
+
+        def regroup_weights(n, w_rows):
+            w_grouped = packed.tile([P, 2, CH, PACK], BF16, name="w_grouped", align_bytes=64)
+            for m in range(matrices_of(n)):
+                nc.vector.tensor_copy(
+                    out=w_grouped[:, m].rearrange("p (c i) j -> p c j i", i=4),
+                    in_=w_rows[:, m].rearrange("p j (c i) -> p c j i", i=4),
+                )
+            return w_grouped
+
+        def quantise_weights(n, w_grouped):
+            w_codes = packed.tile([P, 2, CH], U32, name="w_codes", align_bytes=64)
+            w_scales = packed.tile([P, 2, CH], U8, name="w_scales", align_bytes=64)
+            m = matrices_of(n)
+            nc.vector.quantize_mx(
+                out=w_codes[:, :m].rearrange("p m i -> p (m i)").bitcast(E4M3_X4),
+                scales=w_scales[:, :m].rearrange("p m i -> p (m i)"),
+                in_=w_grouped[:, :m].rearrange("p m i j -> p (m i j)"),
+            )
+            return w_codes, w_scales
+
+        with tc.tile_pool(name="grad", bufs=ROW_TILES) as grad, tc.tile_pool(
+            name="grad_grouped", bufs=3
+        ) as grad_grouped:
+            grad_rows = []
+            for t in range(ROW_TILES):
+                rows = grad.tile([P, JOINTS * CH], BF16, name="rows")
+                nc.sync.dma_start(out=rows[:], in_=grad_out[t * P : (t + 1) * P, :])
+                grad_rows.append(rows)
+            w_rows_of = {}
+            for n in range(WEIGHT_BUFS):
+                w_rows_of[n] = load_weights(n)
+
+            def quantise_gradient(t, first, grouped):
+                joints = slice(first, first + JOINTS_PER_QUANTISE)
+                nc.vector.quantize_mx(
+                    out=g_codes[:, t, joints, :].rearrange("p n b -> p (n b)").bitcast(E5M2_X4),
+                    scales=g_scales[:, t, joints, :].rearrange("p n b -> p (n b)"),
+                    in_=grouped[:].rearrange("p n b j -> p (n b j)"),
+                )
+
+            waiting = None
+            for t in range(ROW_TILES):
+                words = grad_rows[t][:].bitcast(F32).rearrange("b (n p u) -> b n u p", p=P, u=WORDS)
+                for first in range(0, JOINTS, JOINTS_PER_QUANTISE):
+                    grouped = grad_grouped.tile(
+                        [P, JOINTS_PER_QUANTISE, P, PACK], BF16, name="grouped", align_bytes=64
+                    )
+                    grouped_words = grouped[:].bitcast(F32)
+                    for half in range(JOINTS_PER_QUANTISE // JOINTS_PER_BANK):
+                        bank = psum.tile([P, JOINTS_PER_BANK, WORDS, P], F32, name="bank", tag="bank")
+                        for j in range(JOINTS_PER_BANK):
+                            for u in range(WORDS):
+                                nc.tensor.transpose(
+                                    bank[:, j, u, :],
+                                    words[:, first + half * JOINTS_PER_BANK + j, u, :],
+                                    identity[:],
+                                )
+                        side_by_side = grouped_words[:, half * JOINTS_PER_BANK : (half + 1) * JOINTS_PER_BANK]
+                        planes = bank[:].rearrange("p j u b -> p j b u")
+                        if half == 0:
+                            nc.vector.tensor_copy(out=side_by_side, in_=planes)
+                        else:
+                            nc.scalar.copy(out=side_by_side, in_=planes)
+                    if waiting is not None:
+                        quantise_gradient(*waiting)
+                    waiting = (t, first, grouped)
+            quantise_gradient(*waiting)
+
+        with tc.tile_pool(
+            name="result", bufs=ROW_TILES * JOINTS // JOINTS_PER_STORE, reuse_waits="tile"
+        ) as result:
+            w_grouped_of = {0: regroup_weights(0, w_rows_of[0])}
+            out_rows = []
+            for n in range(JOINTS):
+                if n + WEIGHT_BUFS < JOINTS:
+                    w_rows_of[n + WEIGHT_BUFS] = load_weights(n + WEIGHT_BUFS)
+                if n < LAST:
+                    w_grouped_of[n + 1] = regroup_weights(n + 1, w_rows_of[n + 1])
+                w_codes, w_scales = quantise_weights(n, w_grouped_of[n])
+
+                place = n % JOINTS_PER_STORE
+                if place == 0:
+                    out_rows = [
+                        result.tile([P, JOINTS_PER_STORE * CH], F32, name="out_rows")
+                        for t in range(ROW_TILES)
+                    ]
+                for t in range(ROW_TILES):
+                    acc = psum.tile([P, CH], F32, name="acc", tag="bank")
+                    nc.tensor.matmul_mx(
+                        out=acc[:],
+                        lhsT=g_codes[:, t, n, :].bitcast(E5M2_X4),
+                        lhsT_scale=g_scales[:, t, n, :],
+                        rhs=w_codes[:, 0, :].bitcast(E4M3_X4),
+                        rhs_scale=w_scales[:, 0, :],
+                        start=True,
+                        stop=(n == LAST),
+                    )
+                    if n < LAST:
+                        nc.tensor.matmul_mx(
+                            out=acc[:],
+                            lhsT=g_codes[:, t, n + 1, :].bitcast(E5M2_X4),
+                            lhsT_scale=g_scales[:, t, n + 1, :],
+                            rhs=w_codes[:, 1, :].bitcast(E4M3_X4),
+                            rhs_scale=w_scales[:, 1, :],
+                            start=False,
+                            stop=True,
+                        )
+                    nc.scalar.copy(out=out_rows[t][:, place * CH : (place + 1) * CH], in_=acc[:])
+                    if place == JOINTS_PER_STORE - 1:
+                        first_column = (n - place) * CH
+                        nc.sync.dma_start(
+                            out=out[t * P : (t + 1) * P, first_column : first_column + JOINTS_PER_STORE * CH],
+                            in_=out_rows[t][:],
+                        )
+
+
+def matrices_of(n):
+    return 2 if n < LAST else 1

@@ -20,28 +20,37 @@ WORDS = PACK // 2
 JOINTS_PER_BANK = 2
 JOINTS_PER_QUANTISE = 4
 JOINTS_PER_STORE = 2
-WEIGHT_BUFS = 8
+AHEAD = ROW_TILES
+RAW_BUFS = 7
 
 FLOPS = 2 * BATCH * CH * CH * (2 * JOINTS - 1)
 BYTES = 2 * BATCH * JOINTS * CH + 2 * (2 * JOINTS - 1) * CH * CH + 4 * BATCH * JOINTS * CH
+
+
+def matrices_of(n):
+    return 2 if n < LAST else 1
 
 
 def tile_skeletonlinear_pa_kernel(tc, x, w_self, w_parent, bias, grad_out, out):
     nc = tc.nc
 
     with tc.tile_pool(name="keep", bufs=1) as keep, tc.tile_pool(
-        name="weights", bufs=WEIGHT_BUFS
-    ) as weights, tc.tile_pool(name="packed", bufs=3) as packed, tc.psum_pool(
-        name="psum", bufs=8
-    ) as psum:
+        name="raw", bufs=RAW_BUFS
+    ) as raw, tc.tile_pool(name="regrouped", bufs=2) as regrouped, tc.tile_pool(
+        name="packed", bufs=AHEAD + 1
+    ) as packed, tc.psum_pool(name="psum", bufs=8) as psum:
         identity = keep.tile([P, P], F32)
         make_identity(nc, identity[:])
 
         g_codes = keep.tile([P, ROW_TILES, JOINTS, P], U32, align_bytes=64)
         g_scales = keep.tile([P, ROW_TILES, JOINTS, P], U8, align_bytes=64)
 
+        w_rows_of = {}
+        w_grouped_of = {}
+        w_packed_of = {}
+
         def load_weights(n):
-            w_rows = weights.tile([P, 2, PACK, CH], BF16, name="w_rows")
+            w_rows = raw.tile([P, 2, PACK, CH], BF16, name="w_rows")
             nc.sync.dma_start(
                 out=w_rows[:, 0], in_=w_self[n].rearrange("(p j) i -> p j i", j=PACK)
             )
@@ -49,27 +58,35 @@ def tile_skeletonlinear_pa_kernel(tc, x, w_self, w_parent, bias, grad_out, out):
                 nc.sync.dma_start(
                     out=w_rows[:, 1], in_=w_parent[n].rearrange("(p j) i -> p j i", j=PACK)
                 )
-            return w_rows
+            w_rows_of[n] = w_rows
 
-        def regroup_weights(n, w_rows):
-            w_grouped = packed.tile([P, 2, CH, PACK], BF16, name="w_grouped", align_bytes=64)
+        def regroup_weights(n):
+            w_grouped = regrouped.tile([P, 2, CH, PACK], BF16, name="w_grouped", align_bytes=64)
             for m in range(matrices_of(n)):
                 nc.vector.tensor_copy(
                     out=w_grouped[:, m].rearrange("p (c i) j -> p c j i", i=4),
-                    in_=w_rows[:, m].rearrange("p j (c i) -> p c j i", i=4),
+                    in_=w_rows_of[n][:, m].rearrange("p j (c i) -> p c j i", i=4),
                 )
-            return w_grouped
+            w_grouped_of[n] = w_grouped
 
-        def quantise_weights(n, w_grouped):
+        def quantise_weights(n):
             w_codes = packed.tile([P, 2, CH], U32, name="w_codes", align_bytes=64)
             w_scales = packed.tile([P, 2, CH], U8, name="w_scales", align_bytes=64)
             m = matrices_of(n)
             nc.vector.quantize_mx(
                 out=w_codes[:, :m].rearrange("p m i -> p (m i)").bitcast(E4M3_X4),
                 scales=w_scales[:, :m].rearrange("p m i -> p (m i)"),
-                in_=w_grouped[:, :m].rearrange("p m i j -> p (m i j)"),
+                in_=w_grouped_of[n][:, :m].rearrange("p m i j -> p (m i j)"),
             )
-            return w_codes, w_scales
+            w_packed_of[n] = (w_codes, w_scales)
+
+        def prepare_weights(step):
+            if step < JOINTS:
+                regroup_weights(step)
+            if step + RAW_BUFS < JOINTS:
+                load_weights(step + RAW_BUFS)
+            if 1 <= step <= JOINTS:
+                quantise_weights(step - 1)
 
         with tc.tile_pool(name="grad", bufs=ROW_TILES) as grad, tc.tile_pool(
             name="grad_grouped", bufs=3
@@ -79,19 +96,10 @@ def tile_skeletonlinear_pa_kernel(tc, x, w_self, w_parent, bias, grad_out, out):
                 rows = grad.tile([P, JOINTS * CH], BF16, name="rows")
                 nc.sync.dma_start(out=rows[:], in_=grad_out[t * P : (t + 1) * P, :])
                 grad_rows.append(rows)
-            w_rows_of = {}
-            for n in range(WEIGHT_BUFS):
-                w_rows_of[n] = load_weights(n)
+                load_weights(t)
+            for n in range(ROW_TILES, RAW_BUFS):
+                load_weights(n)
 
-            def quantise_gradient(t, first, grouped):
-                joints = slice(first, first + JOINTS_PER_QUANTISE)
-                nc.vector.quantize_mx(
-                    out=g_codes[:, t, joints, :].rearrange("p n b -> p (n b)").bitcast(E5M2_X4),
-                    scales=g_scales[:, t, joints, :].rearrange("p n b -> p (n b)"),
-                    in_=grouped[:].rearrange("p n b j -> p (n b j)"),
-                )
-
-            waiting = None
             for t in range(ROW_TILES):
                 words = grad_rows[t][:].bitcast(F32).rearrange("b (n p u) -> b n u p", p=P, u=WORDS)
                 for first in range(0, JOINTS, JOINTS_PER_QUANTISE):
@@ -99,37 +107,32 @@ def tile_skeletonlinear_pa_kernel(tc, x, w_self, w_parent, bias, grad_out, out):
                         [P, JOINTS_PER_QUANTISE, P, PACK], BF16, name="grouped", align_bytes=64
                     )
                     grouped_words = grouped[:].bitcast(F32)
-                    for half in range(JOINTS_PER_QUANTISE // JOINTS_PER_BANK):
+                    for low in range(0, JOINTS_PER_QUANTISE, JOINTS_PER_BANK):
                         bank = psum.tile([P, JOINTS_PER_BANK, WORDS, P], F32, name="bank", tag="bank")
                         for j in range(JOINTS_PER_BANK):
                             for u in range(WORDS):
                                 nc.tensor.transpose(
-                                    bank[:, j, u, :],
-                                    words[:, first + half * JOINTS_PER_BANK + j, u, :],
-                                    identity[:],
+                                    bank[:, j, u, :], words[:, first + low + j, u, :], identity[:]
                                 )
-                        side_by_side = grouped_words[:, half * JOINTS_PER_BANK : (half + 1) * JOINTS_PER_BANK]
-                        planes = bank[:].rearrange("p j u b -> p j b u")
-                        if half == 0:
-                            nc.vector.tensor_copy(out=side_by_side, in_=planes)
-                        else:
-                            nc.scalar.copy(out=side_by_side, in_=planes)
-                    if waiting is not None:
-                        quantise_gradient(*waiting)
-                    waiting = (t, first, grouped)
-            quantise_gradient(*waiting)
+                        nc.scalar.copy(
+                            out=grouped_words[:, low : low + JOINTS_PER_BANK],
+                            in_=bank[:].rearrange("p j u b -> p j b u"),
+                        )
+                    joints = slice(first, first + JOINTS_PER_QUANTISE)
+                    nc.vector.quantize_mx(
+                        out=g_codes[:, t, joints, :].rearrange("p n b -> p (n b)").bitcast(E5M2_X4),
+                        scales=g_scales[:, t, joints, :].rearrange("p n b -> p (n b)"),
+                        in_=grouped[:].rearrange("p n b j -> p (n b j)"),
+                    )
+                prepare_weights(t)
 
         with tc.tile_pool(
             name="result", bufs=ROW_TILES * JOINTS // JOINTS_PER_STORE, reuse_waits="tile"
         ) as result:
-            w_grouped_of = {0: regroup_weights(0, w_rows_of[0])}
             out_rows = []
             for n in range(JOINTS):
-                if n + WEIGHT_BUFS < JOINTS:
-                    w_rows_of[n + WEIGHT_BUFS] = load_weights(n + WEIGHT_BUFS)
-                if n < LAST:
-                    w_grouped_of[n + 1] = regroup_weights(n + 1, w_rows_of[n + 1])
-                w_codes, w_scales = quantise_weights(n, w_grouped_of[n])
+                prepare_weights(n + AHEAD)
+                w_codes, w_scales = w_packed_of[n]
 
                 place = n % JOINTS_PER_STORE
                 if place == 0:
@@ -165,7 +168,3 @@ def tile_skeletonlinear_pa_kernel(tc, x, w_self, w_parent, bias, grad_out, out):
                             out=out[t * P : (t + 1) * P, first_column : first_column + JOINTS_PER_STORE * CH],
                             in_=out_rows[t][:],
                         )
-
-
-def matrices_of(n):
-    return 2 if n < LAST else 1

@@ -93,14 +93,15 @@ def tile_skeletonlinear_pa_kernel(tc, x, w_self, w_parent, bias, grad_out, out):
         ) as grad_grouped:
             grad_rows = []
             for t in range(ROW_TILES):
+                load_weights(t)
                 rows = grad.tile([P, JOINTS * CH], BF16, name="rows")
                 nc.sync.dma_start(out=rows[:], in_=grad_out[t * P : (t + 1) * P, :])
                 grad_rows.append(rows)
-                load_weights(t)
             for n in range(ROW_TILES, RAW_BUFS):
                 load_weights(n)
 
             for t in range(ROW_TILES):
+                prepare_weights(t)
                 words = grad_rows[t][:].bitcast(F32).rearrange("b (n p u) -> b n u p", p=P, u=WORDS)
                 for first in range(0, JOINTS, JOINTS_PER_QUANTISE):
                     grouped = grad_grouped.tile(
@@ -124,7 +125,6 @@ def tile_skeletonlinear_pa_kernel(tc, x, w_self, w_parent, bias, grad_out, out):
                         scales=g_scales[:, t, joints, :].rearrange("p n b -> p (n b)"),
                         in_=grouped[:].rearrange("p n b j -> p (n b j)"),
                     )
-                prepare_weights(t)
 
         with tc.tile_pool(
             name="result", bufs=ROW_TILES * JOINTS // JOINTS_PER_STORE, reuse_waits="tile"

@@ -19,7 +19,7 @@ LAST = JOINTS - 1
 WORDS = PACK // 2
 JOINTS_PER_BANK = 2
 JOINTS_PER_QUANTISE = 4
-JOINTS_PER_STORE = 2
+JOINTS_PER_STORE = 3
 AHEAD = ROW_TILES
 RAW_BUFS = 7
 

@@ -19,7 +19,7 @@ LAST = JOINTS - 1
 WORDS = PACK // 2
 JOINTS_PER_BANK = 2
 JOINTS_PER_QUANTISE = 4
-JOINTS_PER_STORE = 3
+STORES = ((0, 3), (3, 6), (6, 9), (9, 11), (11, 12))
 AHEAD = ROW_TILES
 RAW_BUFS = 7
 
@@ -126,45 +126,36 @@ def tile_skeletonlinear_pa_kernel(tc, x, w_self, w_parent, bias, grad_out, out):
                         in_=grouped[:].rearrange("p n b j -> p (n b j)"),
                     )
 
-        with tc.tile_pool(
-            name="result", bufs=ROW_TILES * JOINTS // JOINTS_PER_STORE, reuse_waits="tile"
-        ) as result:
-            out_rows = []
-            for n in range(JOINTS):
-                prepare_weights(n + AHEAD)
-                w_codes, w_scales = w_packed_of[n]
-
-                place = n % JOINTS_PER_STORE
-                if place == 0:
-                    out_rows = [
-                        result.tile([P, JOINTS_PER_STORE * CH], F32, name="out_rows")
-                        for t in range(ROW_TILES)
-                    ]
-                for t in range(ROW_TILES):
-                    acc = psum.tile([P, CH], F32, name="acc", tag="bank")
-                    nc.tensor.matmul_mx(
-                        out=acc[:],
-                        lhsT=g_codes[:, t, n, :].bitcast(E5M2_X4),
-                        lhsT_scale=g_scales[:, t, n, :],
-                        rhs=w_codes[:, 0, :].bitcast(E4M3_X4),
-                        rhs_scale=w_scales[:, 0, :],
-                        start=True,
-                        stop=(n == LAST),
-                    )
-                    if n < LAST:
+        with tc.tile_pool(name="result", bufs=1, reuse_waits="tile") as result:
+            out_by_partition = out.rearrange("(t p) c -> p t c", p=P)
+            for first, behind in STORES:
+                out_rows = result.tile(
+                    [P, ROW_TILES, (behind - first) * CH], F32, name="out_rows_%d" % first
+                )
+                for n in range(first, behind):
+                    prepare_weights(n + AHEAD)
+                    w_codes, w_scales = w_packed_of[n]
+                    place = n - first
+                    for t in range(ROW_TILES):
+                        acc = psum.tile([P, CH], F32, name="acc", tag="bank")
                         nc.tensor.matmul_mx(
                             out=acc[:],
-                            lhsT=g_codes[:, t, n + 1, :].bitcast(E5M2_X4),
-                            lhsT_scale=g_scales[:, t, n + 1, :],
-                            rhs=w_codes[:, 1, :].bitcast(E4M3_X4),
-                            rhs_scale=w_scales[:, 1, :],
-                            start=False,
-                            stop=True,
+                            lhsT=g_codes[:, t, n, :].bitcast(E5M2_X4),
+                            lhsT_scale=g_scales[:, t, n, :],
+                            rhs=w_codes[:, 0, :].bitcast(E4M3_X4),
+                            rhs_scale=w_scales[:, 0, :],
+                            start=True,
+                            stop=(n == LAST),
                         )
-                    nc.scalar.copy(out=out_rows[t][:, place * CH : (place + 1) * CH], in_=acc[:])
-                    if place == JOINTS_PER_STORE - 1:
-                        first_column = (n - place) * CH
-                        nc.sync.dma_start(
-                            out=out[t * P : (t + 1) * P, first_column : first_column + JOINTS_PER_STORE * CH],
-                            in_=out_rows[t][:],
-                        )
+                        if n < LAST:
+                            nc.tensor.matmul_mx(
+                                out=acc[:],
+                                lhsT=g_codes[:, t, n + 1, :].bitcast(E5M2_X4),
+                                lhsT_scale=g_scales[:, t, n + 1, :],
+                                rhs=w_codes[:, 1, :].bitcast(E4M3_X4),
+                                rhs_scale=w_scales[:, 1, :],
+                                start=False,
+                                stop=True,
+                            )
+                        nc.scalar.copy(out=out_rows[:, t, place * CH : (place + 1) * CH], in_=acc[:])
+                nc.sync.dma_start(out=out_by_partition[:, :, first * CH : behind * CH], in_=out_rows[:])

@@ -19,7 +19,8 @@ LAST = JOINTS - 1
 WORDS = PACK // 2
 JOINTS_PER_BANK = 2
 JOINTS_PER_QUANTISE = 4
-STORES = ((0, 3), (3, 6), (6, 9), (9, 11), (11, 12))
+STORES = ((0, 5), (5, 9), (9, 12))
+ON_SCALAR = ()
 AHEAD = ROW_TILES
 RAW_BUFS = 7
 
@@ -63,10 +64,12 @@ def tile_skeletonlinear_pa_kernel(tc, x, w_self, w_parent, bias, grad_out, out):
         def regroup_weights(n):
             w_grouped = regrouped.tile([P, 2, CH, PACK], BF16, name="w_grouped", align_bytes=64)
             for m in range(matrices_of(n)):
-                nc.vector.tensor_copy(
-                    out=w_grouped[:, m].rearrange("p (c i) j -> p c j i", i=4),
-                    in_=w_rows_of[n][:, m].rearrange("p j (c i) -> p c j i", i=4),
-                )
+                grouped_view = w_grouped[:, m].rearrange("p (c i) j -> p c j i", i=4)
+                rows_view = w_rows_of[n][:, m].rearrange("p j (c i) -> p c j i", i=4)
+                if (n, m) in ON_SCALAR:
+                    nc.scalar.copy(out=grouped_view, in_=rows_view)
+                else:
+                    nc.vector.tensor_copy(out=grouped_view, in_=rows_view)
             w_grouped_of[n] = w_grouped
 
         def quantise_weights(n):
@@ -81,12 +84,66 @@ def tile_skeletonlinear_pa_kernel(tc, x, w_self, w_parent, bias, grad_out, out):
             w_packed_of[n] = (w_codes, w_scales)
 
         def prepare_weights(step):
+            if step == LAST:
+                quantise_weights(step - 1)
+                regroup_weights(step)
+                return
             if step < JOINTS:
                 regroup_weights(step)
             if step + RAW_BUFS < JOINTS:
                 load_weights(step + RAW_BUFS)
             if 1 <= step <= JOINTS:
                 quantise_weights(step - 1)
+
+        out_by_partition = out.rearrange("(t p) c -> p t c", p=P)
+        out_rows_of = {}
+        grad_ready = []
+        products_done = set()
+
+        def product(t, n):
+            w_codes, w_scales = w_packed_of[n]
+            acc = psum.tile([P, CH], F32, name="acc", tag="bank")
+            nc.tensor.matmul_mx(
+                out=acc[:],
+                lhsT=g_codes[:, t, n, :].bitcast(E5M2_X4),
+                lhsT_scale=g_scales[:, t, n, :],
+                rhs=w_codes[:, 0, :].bitcast(E4M3_X4),
+                rhs_scale=w_scales[:, 0, :],
+                start=True,
+                stop=(n == LAST),
+            )
+            if n < LAST:
+                nc.tensor.matmul_mx(
+                    out=acc[:],
+                    lhsT=g_codes[:, t, n + 1, :].bitcast(E5M2_X4),
+                    lhsT_scale=g_scales[:, t, n + 1, :],
+                    rhs=w_codes[:, 1, :].bitcast(E4M3_X4),
+                    rhs_scale=w_scales[:, 1, :],
+                    start=False,
+                    stop=True,
+                )
+            for index, (first, behind) in enumerate(STORES):
+                if first <= n < behind:
+                    place = out_rows_of[index][:, t, (n - first) * CH : (n - first + 1) * CH]
+                    if n == LAST and t % 2 == 1:
+                        nc.vector.tensor_copy(out=place, in_=acc[:])
+                    else:
+                        nc.scalar.copy(out=place, in_=acc[:])
+                    products_done.add((t, n))
+                    if all((u, k) in products_done for u in range(ROW_TILES) for k in range(first, behind)):
+                        nc.sync.dma_start(
+                            out=out_by_partition[:, :, first * CH : behind * CH],
+                            in_=out_rows_of[index][:],
+                        )
+
+        def products_that_can_run():
+            for n in range(JOINTS):
+                for t in range(ROW_TILES):
+                    if n in w_packed_of and t in grad_ready and (t, n) not in products_done:
+                        product(t, n)
+
+        first_store_width = (STORES[0][1] - STORES[0][0]) * CH
+        out_rows_of[0] = keep.tile([P, ROW_TILES, first_store_width], F32, name="out_rows_0")
 
         with tc.tile_pool(name="grad", bufs=ROW_TILES) as grad, tc.tile_pool(
             name="grad_grouped", bufs=3
@@ -125,37 +182,15 @@ def tile_skeletonlinear_pa_kernel(tc, x, w_self, w_parent, bias, grad_out, out):
                         scales=g_scales[:, t, joints, :].rearrange("p n b -> p (n b)"),
                         in_=grouped[:].rearrange("p n b j -> p (n b j)"),
                     )
+                grad_ready.append(t)
+                products_that_can_run()
 
         with tc.tile_pool(name="result", bufs=1, reuse_waits="tile") as result:
-            out_by_partition = out.rearrange("(t p) c -> p t c", p=P)
-            for first, behind in STORES:
-                out_rows = result.tile(
-                    [P, ROW_TILES, (behind - first) * CH], F32, name="out_rows_%d" % first
-                )
-                for n in range(first, behind):
-                    prepare_weights(n + AHEAD)
-                    w_codes, w_scales = w_packed_of[n]
-                    place = n - first
-                    for t in range(ROW_TILES):
-                        acc = psum.tile([P, CH], F32, name="acc", tag="bank")
-                        nc.tensor.matmul_mx(
-                            out=acc[:],
-                            lhsT=g_codes[:, t, n, :].bitcast(E5M2_X4),
-                            lhsT_scale=g_scales[:, t, n, :],
-                            rhs=w_codes[:, 0, :].bitcast(E4M3_X4),
-                            rhs_scale=w_scales[:, 0, :],
-                            start=True,
-                            stop=(n == LAST),
-                        )
-                        if n < LAST:
-                            nc.tensor.matmul_mx(
-                                out=acc[:],
-                                lhsT=g_codes[:, t, n + 1, :].bitcast(E5M2_X4),
-                                lhsT_scale=g_scales[:, t, n + 1, :],
-                                rhs=w_codes[:, 1, :].bitcast(E4M3_X4),
-                                rhs_scale=w_scales[:, 1, :],
-                                start=False,
-                                stop=True,
-                            )
-                        nc.scalar.copy(out=out_rows[:, t, place * CH : (place + 1) * CH], in_=acc[:])
-                nc.sync.dma_start(out=out_by_partition[:, :, first * CH : behind * CH], in_=out_rows[:])
+            for index, (first, behind) in enumerate(STORES):
+                if index > 0:
+                    out_rows_of[index] = result.tile(
+                        [P, ROW_TILES, (behind - first) * CH], F32, name="out_rows_%d" % index
+                    )
+            for step in range(AHEAD, JOINTS + 1):
+                prepare_weights(step)
+                products_that_can_run()

@@ -19,7 +19,7 @@ LAST = JOINTS - 1
 WORDS = PACK // 2
 JOINTS_PER_BANK = 2
 JOINTS_PER_QUANTISE = 4
-STORES = ((0, 5), (5, 9), (9, 12))
+STORES = ((0, 5), (5, 8), (8, 10), (10, 12))
 ON_SCALAR = ()
 AHEAD = ROW_TILES
 RAW_BUFS = 7

@@ -19,10 +19,11 @@ LAST = JOINTS - 1
 WORDS = PACK // 2
 JOINTS_PER_BANK = 2
 JOINTS_PER_QUANTISE = 4
-STORES = ((0, 5), (5, 8), (8, 10), (10, 12))
-ON_SCALAR = ()
+STORES = ((0, 4), (4, 7), (7, 9), (9, 11), (11, 12))
 AHEAD = ROW_TILES
-RAW_BUFS = 7
+QUAD = 4
+RAW_QUADS = 2
+WEIGHT_LOADS = ((0, 1), (1, 2), (2, 3), (3, 4), (4, 6), (6, 8), (8, 12))
 
 FLOPS = 2 * BATCH * CH * CH * (2 * JOINTS - 1)
 BYTES = 2 * BATCH * JOINTS * CH + 2 * (2 * JOINTS - 1) * CH * CH + 4 * BATCH * JOINTS * CH
@@ -36,7 +37,7 @@ def tile_skeletonlinear_pa_kernel(tc, x, w_self, w_parent, bias, grad_out, out):
     nc = tc.nc
 
     with tc.tile_pool(name="keep", bufs=1) as keep, tc.tile_pool(
-        name="raw", bufs=RAW_BUFS
+        name="raw", bufs=RAW_QUADS
     ) as raw, tc.tile_pool(name="regrouped", bufs=2) as regrouped, tc.tile_pool(
         name="packed", bufs=AHEAD + 1
     ) as packed, tc.psum_pool(name="psum", bufs=8) as psum:
@@ -46,31 +47,27 @@ def tile_skeletonlinear_pa_kernel(tc, x, w_self, w_parent, bias, grad_out, out):
         g_codes = keep.tile([P, ROW_TILES, JOINTS, P], U32, align_bytes=64)
         g_scales = keep.tile([P, ROW_TILES, JOINTS, P], U8, align_bytes=64)
 
-        w_rows_of = {}
+        quad_rows_of = {}
         w_grouped_of = {}
         w_packed_of = {}
 
-        def load_weights(n):
-            w_rows = raw.tile([P, 2, PACK, CH], BF16, name="w_rows")
-            nc.sync.dma_start(
-                out=w_rows[:, 0], in_=w_self[n].rearrange("(p j) i -> p j i", j=PACK)
-            )
-            if n < LAST:
+        def load_weights(first, behind):
+            quad = first // QUAD
+            if quad not in quad_rows_of:
+                quad_rows_of[quad] = raw.tile([P, 2, QUAD, PACK, CH], BF16, name="quad_rows")
+            for m, stack, end in ((0, w_self, behind), (1, w_parent, min(behind, LAST))):
                 nc.sync.dma_start(
-                    out=w_rows[:, 1], in_=w_parent[n].rearrange("(p j) i -> p j i", j=PACK)
+                    out=quad_rows_of[quad][:, m, first % QUAD : first % QUAD + end - first],
+                    in_=stack[first:end].rearrange("k (p j) i -> p k j i", j=PACK),
                 )
-            w_rows_of[n] = w_rows
 
-        def regroup_weights(n):
-            w_grouped = regrouped.tile([P, 2, CH, PACK], BF16, name="w_grouped", align_bytes=64)
-            for m in range(matrices_of(n)):
-                grouped_view = w_grouped[:, m].rearrange("p (c i) j -> p c j i", i=4)
-                rows_view = w_rows_of[n][:, m].rearrange("p j (c i) -> p c j i", i=4)
-                if (n, m) in ON_SCALAR:
-                    nc.scalar.copy(out=grouped_view, in_=rows_view)
-                else:
-                    nc.vector.tensor_copy(out=grouped_view, in_=rows_view)
-            w_grouped_of[n] = w_grouped
+        def regroup_weights(n, m):
+            if m == 0:
+                w_grouped_of[n] = regrouped.tile([P, 2, CH, PACK], BF16, name="w_grouped", align_bytes=64)
+            nc.vector.tensor_copy(
+                out=w_grouped_of[n][:, m].rearrange("p (c i) j -> p c j i", i=4),
+                in_=quad_rows_of[n // QUAD][:, m, n % QUAD].rearrange("p j (c i) -> p c j i", i=4),
+            )
 
         def quantise_weights(n):
             w_codes = packed.tile([P, 2, CH], U32, name="w_codes", align_bytes=64)
@@ -86,14 +83,18 @@ def tile_skeletonlinear_pa_kernel(tc, x, w_self, w_parent, bias, grad_out, out):
         def prepare_weights(step):
             if step == LAST:
                 quantise_weights(step - 1)
-                regroup_weights(step)
+                regroup_weights(step, 0)
                 return
             if step < JOINTS:
-                regroup_weights(step)
-            if step + RAW_BUFS < JOINTS:
-                load_weights(step + RAW_BUFS)
+                regroup_weights(step, 0)
             if 1 <= step <= JOINTS:
                 quantise_weights(step - 1)
+            if step < LAST:
+                regroup_weights(step, 1)
+            if step % QUAD == QUAD - 1:
+                for first, behind in WEIGHT_LOADS:
+                    if first // QUAD == step // QUAD + RAW_QUADS:
+                        load_weights(first, behind)
 
         out_by_partition = out.rearrange("(t p) c -> p t c", p=P)
         out_rows_of = {}
@@ -149,13 +150,17 @@ def tile_skeletonlinear_pa_kernel(tc, x, w_self, w_parent, bias, grad_out, out):
             name="grad_grouped", bufs=3
         ) as grad_grouped:
             grad_rows = []
-            for t in range(ROW_TILES):
-                load_weights(t)
+
+            def load_gradient(t):
                 rows = grad.tile([P, JOINTS * CH], BF16, name="rows")
                 nc.sync.dma_start(out=rows[:], in_=grad_out[t * P : (t + 1) * P, :])
                 grad_rows.append(rows)
-            for n in range(ROW_TILES, RAW_BUFS):
-                load_weights(n)
+
+            for index, (first, behind) in enumerate(WEIGHT_LOADS):
+                if first // QUAD < RAW_QUADS:
+                    load_weights(first, behind)
+                    if index < ROW_TILES:
+                        load_gradient(index)
 
             for t in range(ROW_TILES):
                 prepare_weights(t)

@@ -21,6 +21,7 @@ JOINTS_PER_BANK = 2
 JOINTS_PER_QUANTISE = 4
 STORES = ((0, 4), (4, 7), (7, 9), (9, 11), (11, 12))
 AHEAD = ROW_TILES
+DMA_ALIGN = 256
 QUAD = 4
 RAW_QUADS = 2
 WEIGHT_LOADS = ((0, 1), (1, 2), (2, 3), (3, 4), (4, 6), (6, 8), (8, 12))
@@ -54,7 +55,7 @@ def tile_skeletonlinear_pa_kernel(tc, x, w_self, w_parent, bias, grad_out, out):
         def load_weights(first, behind):
             quad = first // QUAD
             if quad not in quad_rows_of:
-                quad_rows_of[quad] = raw.tile([P, 2, QUAD, PACK, CH], BF16, name="quad_rows")
+                quad_rows_of[quad] = raw.tile([P, 2, QUAD, PACK, CH], BF16, name="quad_rows", align_bytes=DMA_ALIGN)
             for m, stack, end in ((0, w_self, behind), (1, w_parent, min(behind, LAST))):
                 nc.sync.dma_start(
                     out=quad_rows_of[quad][:, m, first % QUAD : first % QUAD + end - first],
@@ -144,7 +145,9 @@ def tile_skeletonlinear_pa_kernel(tc, x, w_self, w_parent, bias, grad_out, out):
                         product(t, n)
 
         first_store_width = (STORES[0][1] - STORES[0][0]) * CH
-        out_rows_of[0] = keep.tile([P, ROW_TILES, first_store_width], F32, name="out_rows_0")
+        out_rows_of[0] = keep.tile(
+            [P, ROW_TILES, first_store_width], F32, name="out_rows_0", align_bytes=DMA_ALIGN
+        )
 
         with tc.tile_pool(name="grad", bufs=ROW_TILES) as grad, tc.tile_pool(
             name="grad_grouped", bufs=3
@@ -152,7 +155,7 @@ def tile_skeletonlinear_pa_kernel(tc, x, w_self, w_parent, bias, grad_out, out):
             grad_rows = []
 
             def load_gradient(t):
-                rows = grad.tile([P, JOINTS * CH], BF16, name="rows")
+                rows = grad.tile([P, JOINTS * CH], BF16, name="rows", align_bytes=DMA_ALIGN)
                 nc.sync.dma_start(out=rows[:], in_=grad_out[t * P : (t + 1) * P, :])
                 grad_rows.append(rows)
 
@@ -194,7 +197,7 @@ def tile_skeletonlinear_pa_kernel(tc, x, w_self, w_parent, bias, grad_out, out):
             for index, (first, behind) in enumerate(STORES):
                 if index > 0:
                     out_rows_of[index] = result.tile(
-                        [P, ROW_TILES, (behind - first) * CH], F32, name="out_rows_%d" % index
+                        [P, ROW_TILES, (behind - first) * CH], F32, name="out_rows_%d" % index, align_bytes=DMA_ALIGN
                     )
             for step in range(AHEAD, JOINTS + 1):
                 prepare_weights(step)

@@ -21,7 +21,7 @@ JOINTS_PER_BANK = 2
 JOINTS_PER_QUANTISE = 4
 STORES = ((0, 4), (4, 7), (7, 9), (9, 11), (11, 12))
 AHEAD = ROW_TILES
-DMA_ALIGN = 256
+DMA_ALIGN = 1024
 QUAD = 4
 RAW_QUADS = 2
 WEIGHT_LOADS = ((0, 1), (1, 2), (2, 3), (3, 4), (4, 6), (6, 8), (8, 12))

@@ -21,7 +21,7 @@ JOINTS_PER_BANK = 2
 JOINTS_PER_QUANTISE = 4
 STORES = ((0, 4), (4, 7), (7, 9), (9, 11), (11, 12))
 AHEAD = ROW_TILES
-DMA_ALIGN = 1024
+DMA_ALIGN = 4096
 QUAD = 4
 RAW_QUADS = 2
 WEIGHT_LOADS = ((0, 1), (1, 2), (2, 3), (3, 4), (4, 6), (6, 8), (8, 12))
@@ -135,7 +135,7 @@ def tile_skeletonlinear_pa_kernel(tc, x, w_self, w_parent, bias, grad_out, out):
                     if all((u, k) in products_done for u in range(ROW_TILES) for k in range(first, behind)):
                         nc.sync.dma_start(
                             out=out_by_partition[:, :, first * CH : behind * CH],
-                            in_=out_rows_of[index][:],
+                            in_=out_rows_of[index],
                         )
 
         def products_that_can_run():
@@ -145,9 +145,10 @@ def tile_skeletonlinear_pa_kernel(tc, x, w_self, w_parent, bias, grad_out, out):
                         product(t, n)
 
         first_store_width = (STORES[0][1] - STORES[0][0]) * CH
-        out_rows_of[0] = keep.tile(
+        first_out_rows = keep.tile(
             [P, ROW_TILES, first_store_width], F32, name="out_rows_0", align_bytes=DMA_ALIGN
         )
+        out_rows_of[0] = first_out_rows[:]
 
         with tc.tile_pool(name="grad", bufs=ROW_TILES) as grad, tc.tile_pool(
             name="grad_grouped", bufs=3
@@ -194,11 +195,22 @@ def tile_skeletonlinear_pa_kernel(tc, x, w_self, w_parent, bias, grad_out, out):
                 products_that_can_run()
 
         with tc.tile_pool(name="result", bufs=1, reuse_waits="tile") as result:
-            for index, (first, behind) in enumerate(STORES):
-                if index > 0:
-                    out_rows_of[index] = result.tile(
-                        [P, ROW_TILES, (behind - first) * CH], F32, name="out_rows_%d" % index, align_bytes=DMA_ALIGN
-                    )
+            middle = STORES[1:-1]
+            middle_rows = result.tile(
+                [P, ROW_TILES * (middle[-1][1] - middle[0][0]) * CH], F32, name="middle_rows", align_bytes=DMA_ALIGN
+            )
+            for index, (first, behind) in enumerate(middle):
+                out_rows_of[index + 1] = middle_rows[
+                    :, ROW_TILES * (first - middle[0][0]) * CH : ROW_TILES * (behind - middle[0][0]) * CH
+                ].rearrange("p (t c) -> p t c", t=ROW_TILES)
             for step in range(AHEAD, JOINTS + 1):
+                if step == JOINTS:
+                    last_out_rows = keep.tile(
+                        [P, ROW_TILES, (STORES[-1][1] - STORES[-1][0]) * CH],
+                        F32,
+                        name="out_rows_0",
+                        align_bytes=DMA_ALIGN,
+                    )
+                    out_rows_of[len(STORES) - 1] = last_out_rows[:]
                 prepare_weights(step)
                 products_that_can_run()

import concourse.mybir as mybir
from concourse.masks import make_identity

BF16 = mybir.dt.bfloat16
F32 = mybir.dt.float32
U32 = mybir.dt.uint32
U8 = mybir.dt.uint8
E5M2_X4 = mybir.dt.float8_e5m2_x4
E4M3_X4 = mybir.dt.float8_e4m3fn_x4

P = 128
PACK = 4
BATCH = 512
JOINTS = 12
CH = 512
ROW_TILES = BATCH // P
LAST = JOINTS - 1

WORDS = PACK // 2
JOINTS_PER_BANK = 2
JOINTS_PER_QUANTISE = 4
STORES = ((0, 4), (4, 7), (7, 9), (9, 11), (11, 12))
AHEAD = ROW_TILES
DMA_ALIGN = 4096
QUAD = 4
RAW_QUADS = 2
WEIGHT_LOADS = ((0, 1), (1, 2), (2, 3), (3, 4), (4, 6), (6, 8), (8, 12))

FLOPS = 2 * BATCH * CH * CH * (2 * JOINTS - 1)
BYTES = 2 * BATCH * JOINTS * CH + 2 * (2 * JOINTS - 1) * CH * CH + 4 * BATCH * JOINTS * CH


def matrices_of(n):
    return 2 if n < LAST else 1


def tile_skeletonlinear_pa_kernel(tc, x, w_self, w_parent, bias, grad_out, out):
    nc = tc.nc

    with tc.tile_pool(name="keep", bufs=1) as keep, tc.tile_pool(
        name="raw", bufs=RAW_QUADS
    ) as raw, tc.tile_pool(name="regrouped", bufs=2) as regrouped, tc.tile_pool(
        name="packed", bufs=AHEAD + 1
    ) as packed, tc.psum_pool(name="psum", bufs=8) as psum:
        identity = keep.tile([P, P], F32)
        make_identity(nc, identity[:])

        g_codes = keep.tile([P, ROW_TILES, JOINTS, P], U32, align_bytes=64)
        g_scales = keep.tile([P, ROW_TILES, JOINTS, P], U8, align_bytes=64)

        quad_rows_of = {}
        w_grouped_of = {}
        w_packed_of = {}

        def load_weights(first, behind):
            quad = first // QUAD
            if quad not in quad_rows_of:
                quad_rows_of[quad] = raw.tile([P, 2, QUAD, PACK, CH], BF16, name="quad_rows", align_bytes=DMA_ALIGN)
            for m, stack, end in ((0, w_self, behind), (1, w_parent, min(behind, LAST))):
                nc.sync.dma_start(
                    out=quad_rows_of[quad][:, m, first % QUAD : first % QUAD + end - first],
                    in_=stack[first:end].rearrange("k (p j) i -> p k j i", j=PACK),
                )

        def regroup_weights(n, m):
            if m == 0:
                w_grouped_of[n] = regrouped.tile([P, 2, CH, PACK], BF16, name="w_grouped", align_bytes=64)
            nc.vector.tensor_copy(
                out=w_grouped_of[n][:, m].rearrange("p (c i) j -> p c j i", i=4),
                in_=quad_rows_of[n // QUAD][:, m, n % QUAD].rearrange("p j (c i) -> p c j i", i=4),
            )

        def quantise_weights(n):
            w_codes = packed.tile([P, 2, CH], U32, name="w_codes", align_bytes=64)
            w_scales = packed.tile([P, 2, CH], U8, name="w_scales", align_bytes=64)
            m = matrices_of(n)
            nc.vector.quantize_mx(
                out=w_codes[:, :m].rearrange("p m i -> p (m i)").bitcast(E4M3_X4),
                scales=w_scales[:, :m].rearrange("p m i -> p (m i)"),
                in_=w_grouped_of[n][:, :m].rearrange("p m i j -> p (m i j)"),
            )
            w_packed_of[n] = (w_codes, w_scales)

        def prepare_weights(step):
            if step == LAST:
                quantise_weights(step - 1)
                regroup_weights(step, 0)
                return
            if step < JOINTS:
                regroup_weights(step, 0)
            if 1 <= step <= JOINTS:
                quantise_weights(step - 1)
            if step < LAST:
                regroup_weights(step, 1)
            if step % QUAD == QUAD - 1:
                for first, behind in WEIGHT_LOADS:
                    if first // QUAD == step // QUAD + RAW_QUADS:
                        load_weights(first, behind)

        out_by_partition = out.rearrange("(t p) c -> p t c", p=P)
        out_rows_of = {}
        grad_ready = []
        products_done = set()

        def product(t, n):
            w_codes, w_scales = w_packed_of[n]
            acc = psum.tile([P, CH], F32, name="acc", tag="bank")
            nc.tensor.matmul_mx(
                out=acc[:],
                lhsT=g_codes[:, t, n, :].bitcast(E5M2_X4),
                lhsT_scale=g_scales[:, t, n, :],
                rhs=w_codes[:, 0, :].bitcast(E4M3_X4),
                rhs_scale=w_scales[:, 0, :],
                start=True,
                stop=(n == LAST),
            )
            if n < LAST:
                nc.tensor.matmul_mx(
                    out=acc[:],
                    lhsT=g_codes[:, t, n + 1, :].bitcast(E5M2_X4),
                    lhsT_scale=g_scales[:, t, n + 1, :],
                    rhs=w_codes[:, 1, :].bitcast(E4M3_X4),
                    rhs_scale=w_scales[:, 1, :],
                    start=False,
                    stop=True,
                )
            for index, (first, behind) in enumerate(STORES):
                if first <= n < behind:
                    place = out_rows_of[index][:, t, (n - first) * CH : (n - first + 1) * CH]
                    if n == LAST and t % 2 == 1:
                        nc.vector.tensor_copy(out=place, in_=acc[:])
                    else:
                        nc.scalar.copy(out=place, in_=acc[:])
                    products_done.add((t, n))
                    if all((u, k) in products_done for u in range(ROW_TILES) for k in range(first, behind)):
                        nc.sync.dma_start(
                            out=out_by_partition[:, :, first * CH : behind * CH],
                            in_=out_rows_of[index],
                        )

        def products_that_can_run():
            for n in range(JOINTS):
                for t in range(ROW_TILES):
                    if n in w_packed_of and t in grad_ready and (t, n) not in products_done:
                        product(t, n)

        first_store_width = (STORES[0][1] - STORES[0][0]) * CH
        first_out_rows = keep.tile(
            [P, ROW_TILES, first_store_width], F32, name="out_rows_0", align_bytes=DMA_ALIGN
        )
        out_rows_of[0] = first_out_rows[:]

        with tc.tile_pool(name="grad", bufs=ROW_TILES) as grad, tc.tile_pool(
            name="grad_grouped", bufs=3
        ) as grad_grouped:
            grad_rows = []

            def load_gradient(t):
                rows = grad.tile([P, JOINTS * CH], BF16, name="rows", align_bytes=DMA_ALIGN)
                nc.sync.dma_start(out=rows[:], in_=grad_out[t * P : (t + 1) * P, :])
                grad_rows.append(rows)

            for index, (first, behind) in enumerate(WEIGHT_LOADS):
                if first // QUAD < RAW_QUADS:
                    load_weights(first, behind)
                    if index < ROW_TILES:
                        load_gradient(index)

            for t in range(ROW_TILES):
                prepare_weights(t)
                words = grad_rows[t][:].bitcast(F32).rearrange("b (n p u) -> b n u p", p=P, u=WORDS)
                for first in range(0, JOINTS, JOINTS_PER_QUANTISE):
                    grouped = grad_grouped.tile(
                        [P, JOINTS_PER_QUANTISE, P, PACK], BF16, name="grouped", align_bytes=64
                    )
                    grouped_words = grouped[:].bitcast(F32)
                    for low in range(0, JOINTS_PER_QUANTISE, JOINTS_PER_BANK):
                        bank = psum.tile([P, JOINTS_PER_BANK, WORDS, P], F32, name="bank", tag="bank")
                        for j in range(JOINTS_PER_BANK):
                            for u in range(WORDS):
                                nc.tensor.transpose(
                                    bank[:, j, u, :], words[:, first + low + j, u, :], identity[:]
                                )
                        nc.scalar.copy(
                            out=grouped_words[:, low : low + JOINTS_PER_BANK],
                            in_=bank[:].rearrange("p j u b -> p j b u"),
                        )
                    joints = slice(first, first + JOINTS_PER_QUANTISE)
                    nc.vector.quantize_mx(
                        out=g_codes[:, t, joints, :].rearrange("p n b -> p (n b)").bitcast(E5M2_X4),
                        scales=g_scales[:, t, joints, :].rearrange("p n b -> p (n b)"),
                        in_=grouped[:].rearrange("p n b j -> p (n b j)"),
                    )
                grad_ready.append(t)
                products_that_can_run()

        with tc.tile_pool(name="result", bufs=1, reuse_waits="tile") as result:
            middle = STORES[1:-1]
            middle_rows = result.tile(
                [P, ROW_TILES * (middle[-1][1] - middle[0][0]) * CH], F32, name="middle_rows", align_bytes=DMA_ALIGN
            )
            for index, (first, behind) in enumerate(middle):
                out_rows_of[index + 1] = middle_rows[
                    :, ROW_TILES * (first - middle[0][0]) * CH : ROW_TILES * (behind - middle[0][0]) * CH
                ].rearrange("p (t c) -> p t c", t=ROW_TILES)
            for step in range(AHEAD, JOINTS + 1):
                if step == JOINTS:
                    last_out_rows = keep.tile(
                        [P, ROW_TILES, (STORES[-1][1] - STORES[-1][0]) * CH],
                        F32,
                        name="out_rows_0",
                        align_bytes=DMA_ALIGN,
                    )
                    out_rows_of[len(STORES) - 1] = last_out_rows[:]
                prepare_weights(step)
                products_that_can_run()
